import numpy as np
import ml_dtypes


def mxq(x, axis, fmt="e4m3"):
    dtype, down = {"e4m3": (ml_dtypes.float8_e4m3fn, 7), "e5m2": (ml_dtypes.float8_e5m2, 14)}[fmt]
    v = np.moveaxis(np.asarray(x, np.float32).astype(ml_dtypes.bfloat16).astype(np.float64), axis, -1)
    blocks = v.reshape(v.shape[:-1] + (-1, 32))
    amax = np.abs(blocks).max(-1, keepdims=True)
    byte = np.maximum(np.where(amax > 0, np.frexp(amax)[1] - 1 + 127, 0) - down, 1)
    scale = np.exp2(byte - 127.0)
    codes = (blocks / scale).astype(np.float32).astype(dtype).astype(np.float64)
    return np.moveaxis((codes * scale).reshape(v.shape), -1, axis)


WIDE = False


def mx_kscale(k):
    if not WIDE:
        return np.ones(k)
    levels = np.array([10, -10, 5, -5, 0])
    a = np.random.permutation(np.resize(levels, k // 512 * 4)).reshape(k // 512, 4)
    idx = np.arange(k)
    return np.exp2(a[idx // 512, idx % 128 // 32])


BF16 = ml_dtypes.bfloat16


def bf(x):
    return np.asarray(x, np.float32).astype(BF16)


def f64(x):
    return np.asarray(x).astype(np.float64)


E2M1 = np.array([0.0, 0.5, 1.0, 1.5, 2.0, 3.0, 4.0, 6.0, -0.0, -0.5, -1.0, -1.5, -2.0, -3.0, -4.0, -6.0])


def pack_weight(w, fmt):
    k, n = w.shape
    w = f64(bf(w)).reshape(k // 32, 32, n)
    amax = np.abs(w).max(1)
    if fmt == "e4m3":
        byte = np.frexp(amax)[1] - 1 + 127 - 7
    else:
        mant, ex = np.frexp(amax / 6.0)
        byte = np.where(mant > 0.5, ex, ex - 1) + 127
    byte = np.clip(np.where(amax > 0, byte, 1), 1, 254)
    scaled = (w * np.exp2(127.0 - byte)[:, None, :]).reshape(k, n).astype(np.float32)
    by_word = np.ascontiguousarray(scaled.reshape(k // 512, 128, 4, n).transpose(0, 1, 3, 2))
    if fmt == "e4m3":
        words = by_word.astype(ml_dtypes.float8_e4m3fn).view(np.uint8)
    else:
        c = by_word.astype(ml_dtypes.float4_e2m1fn).view(np.uint8) & 0xF
        words = c[..., 0::2] | (c[..., 1::2] << 4)
    return np.ascontiguousarray(words), np.ascontiguousarray(byte.astype(np.uint8).reshape(k // 512, 16, n))


def unpack_weight(words, scales, fmt):
    g, p, n, _ = words.shape
    if fmt == "e4m3":
        vals = np.ascontiguousarray(words).view(ml_dtypes.float8_e4m3fn).astype(np.float64)
    else:
        nib = np.empty((g, p, n, 4), np.uint8)
        nib[..., 0::2] = words & 0xF
        nib[..., 1::2] = words >> 4
        vals = E2M1[nib]
    vals = vals * np.repeat(np.exp2(scales.astype(np.float64) - 127.0), 8, axis=1)[..., None]
    return vals.transpose(0, 1, 3, 2).reshape(g * 512, n)

def pack4(w):
    words, scales = pack_weight(w, "e2m1")
    return words.reshape(words.shape[0], 128, -1), scales


def unpack4(words, scales):
    return unpack_weight(words.reshape(words.shape[0], 128, -1, 2), scales, "e2m1")


B, S, D, E = 1, 512, 512, 2
K = E * D


def setup_inputs():
    s = mx_kscale(K)
    att = bf(np.random.standard_normal((E, B, S, D)) * 0.3 * s.reshape(E, 1, 1, D))
    scene_reps = bf(np.random.standard_normal((B, S, D)))
    wo = np.random.standard_normal((D, K)) * 2.0 / np.sqrt(K) / s[None, :]
    words, scales = pack4(wo.T)
    return {"att": att,
            "scene_reps": scene_reps,
            "Wo_words": words,
            "Wo_scales": scales,
            "bo": bf(np.random.standard_normal(D) * 0.1),
            "gamma": bf(1.0 + np.random.standard_normal(D) * 0.1),
            "beta": bf(np.random.standard_normal(D) * 0.1)}


def reference(att, scene_reps, Wo_words, Wo_scales, bo, gamma, beta):
    cat = np.moveaxis(f64(att), 0, 2).reshape(B, S, K)
    fused = (mxq(cat, 2, "e4m3") @ unpack4(Wo_words, Wo_scales)) + f64(bo)
    y = f64(scene_reps) + fused
    mu = y.mean(-1, keepdims=True)
    var = y.var(-1, keepdims=True)
    return (y - mu) / np.sqrt(var + 1e-5) * f64(gamma) + f64(beta)

@@ -1,0 +1,187 @@
+from contextlib import ExitStack
+
+import concourse.mybir as mybir
+from concourse.masks import make_identity
+
+F32 = mybir.dt.float32
+BF16 = mybir.dt.bfloat16
+I32 = mybir.dt.int32
+U32 = mybir.dt.uint32
+U8 = mybir.dt.uint8
+FP8X4 = mybir.dt.float8_e4m3fn_x4
+FP4X4 = mybir.dt.float4_e2m1fn_x4
+ALU = mybir.AluOpType
+ACT = mybir.ActivationFunctionType
+
+P = 128
+S = 512
+D = 512
+E = 2
+ROW_TILES = S // P
+EPS = 1e-5
+
+FLOPS = 2 * S * (E * D) * D
+
+
+def tile_heterogeneousgraphtransformer_pb_s_kernel(
+    tc, att, scene_reps, Wo_words, Wo_scales, bo, gamma, beta, out
+):
+    nc = tc.nc
+    with ExitStack() as ctx:
+        keep = ctx.enter_context(tc.tile_pool(name="keep", bufs=1))
+        psum_rows = ctx.enter_context(tc.psum_pool(name="psum_rows", bufs=1))
+        psum_xt = ctx.enter_context(tc.psum_pool(name="psum_xt", bufs=2))
+        psum_acc = ctx.enter_context(tc.psum_pool(name="psum_acc", bufs=3))
+        ctx.enter_context(tc.manual_schedule())
+
+        bo_rows = keep.tile([P, D], BF16)
+        w_planes = keep.tile([P, E, D], U8, align_bytes=64)
+        gamma_rows = keep.tile([P, D], BF16)
+        beta_rows = keep.tile([P, D], BF16)
+        ones = keep.tile([P, P], BF16)
+        one_col = keep.tile([P, 1], F32)
+        nc.vector.memset(bo_rows[:], 0.0)
+        nc.vector.memset(w_planes[:].rearrange("p g n -> p (g n)").bitcast(I32), 0)
+        nc.vector.memset(ones[:], 1.0)
+        nc.vector.memset(one_col[:], 1.0)
+        nc.vector.memset(gamma_rows[:], 0.0)
+        nc.vector.memset(beta_rows[:], 0.0)
+        ident = keep.tile([P, P], F32)
+        make_identity(nc, ident[:])
+
+        nc.sync.dma_start(out=bo_rows[0:1, :], in_=bo.unsqueeze(0))
+        scale_words = Wo_scales.bitcast(I32)
+        for r in range(4):
+            nc.sync.dma_start(
+                out=w_planes[r:P:32, :, :].bitcast(I32),
+                in_=scale_words[:, r:16:4, :].rearrange("g q w -> q g w"),
+            )
+        nc.gpsimd.dma_start(out=gamma_rows[0:1, :], in_=gamma.unsqueeze(0))
+        nc.gpsimd.dma_start(out=beta_rows[0:1, :], in_=beta.unsqueeze(0))
+
+        w_words = keep.tile([P, E, 2 * D], U8, align_bytes=64)
+        att_sb = []
+        scene_sb = []
+        for i in range(ROW_TILES):
+            rows = slice(i * P, (i + 1) * P)
+            att_i = keep.tile([P, E, D], BF16, name="att%d" % i)
+            nc.sync.dma_start(out=att_i[:], in_=att[:, 0, rows, :].rearrange("e s d -> s e d"))
+            att_sb.append(att_i)
+            if i == 0:
+                nc.sync.dma_start(
+                    out=w_words[:].bitcast(I32),
+                    in_=Wo_words.bitcast(I32).rearrange("g p w -> p g w"),
+                )
+            scene_i = keep.tile([P, D], BF16, name="scene%d" % i)
+            nc.sync.dma_start(out=scene_i[:], in_=scene_reps[0, rows, :])
+            scene_sb.append(scene_i)
+
+        table_warm = keep.tile([P, 1], F32)
+        nc.scalar.activation(out=table_warm[:], in_=one_col[:], func=ACT.Abs_reciprocal_sqrt)
+
+        def spread(rows_tile, name):
+            spread_ps = psum_rows.tile([P, D], F32, name=name)
+            nc.tensor.matmul(out=spread_ps[:], lhsT=ones[:], rhs=rows_tile[:], start=True, stop=True)
+            return spread_ps
+
+        bo_ps = spread(bo_rows, "bo_ps")
+        bo_sb = keep.tile([P, D], BF16)
+        nc.scalar.copy(out=bo_sb[:], in_=bo_ps[:])
+
+        resid = []
+        for i in range(ROW_TILES):
+            resid_i = keep.tile([P, D], F32, name="resid%d" % i)
+            nc.gpsimd.tensor_tensor(out=resid_i[:], in0=scene_sb[i][:], in1=bo_sb[:], op=ALU.add)
+            resid.append(resid_i)
+
+        grouped = {}
+        codes = {}
+        planes = {}
+        acc = {}
+        y = {}
+        negmean = {}
+        rstd = {}
+        scaled = {}
+
+        def transpose_tile(i):
+            xt = psum_xt.tile([P, E, 2, P], F32, name="xt")
+            for g in range(E):
+                words = att_sb[i][:, g, :].bitcast(F32)
+                for u in range(2):
+                    nc.tensor.transpose(xt[:, g, u, :], words[:, u : D // 2 : 2], ident[:])
+            grouped[i] = keep.tile([P, E * P * 4], BF16, name="grouped%d" % i, align_bytes=64)
+            nc.scalar.copy(
+                out=grouped[i][:].bitcast(F32).rearrange("p (g s u) -> p g s u", g=E, u=2),
+                in_=xt[:].rearrange("p g u s -> p g s u"),
+            )
+
+        def quantise_tile(i):
+            codes[i] = keep.tile([P, E * P], U32, name="codes%d" % i, align_bytes=64)
+            planes[i] = keep.tile([P, E * P], U8, name="planes%d" % i, align_bytes=64)
+            nc.vector.quantize_mx(out=codes[i][:].bitcast(FP8X4), scales=planes[i][:], in_=grouped[i][:])
+
+        def multiply_tile(i):
+            acc[i] = psum_acc.tile([P, D], F32, name="acc")
+            for g in range(E):
+                cols = slice(g * P, (g + 1) * P)
+                nc.tensor.matmul_mx(
+                    out=acc[i][:],
+                    lhsT=codes[i][:, cols].bitcast(FP8X4),
+                    lhsT_scale=planes[i][:, cols],
+                    rhs=w_words[:, g, :].bitcast(FP4X4),
+                    rhs_scale=w_planes[:, g, :],
+                    start=(g == 0),
+                    stop=(g == E - 1),
+                )
+
+        def centre_tile(i):
+            y[i] = keep.tile([P, D], F32, name="y%d" % i)
+            y_sum = keep.tile([P, 1], F32, name="ysum%d" % i)
+            nc.vector.scalar_tensor_tensor(
+                out=y[i][:], in0=acc[i][:], scalar=1.0, in1=resid[i][:],
+                op0=ALU.mult, op1=ALU.add, accum_out=y_sum[:],
+            )
+            negmean[i] = keep.tile([P, 1], F32, name="negmean%d" % i)
+            nc.vector.tensor_scalar(
+                out=negmean[i][:], in0=y_sum[:], scalar1=-1.0 / D, scalar2=None, op0=ALU.mult
+            )
+            squares = keep.tile([P, D], F32, name="squares%d" % i)
+            sq_sum = keep.tile([P, 1], F32, name="sqsum%d" % i)
+            nc.scalar.activation(
+                out=squares[:], in_=y[i][:], func=ACT.Square, bias=negmean[i][:], scale=1.0,
+                accum_out=sq_sum[:],
+            )
+            rstd[i] = keep.tile([P, 1], F32, name="rstd%d" % i)
+            nc.scalar.activation(
+                out=rstd[i][:], in_=sq_sum[:], func=ACT.Abs_reciprocal_sqrt, bias=EPS, scale=1.0 / D
+            )
+            scaled[i] = keep.tile([P, D], F32, name="scaled%d" % i)
+            nc.vector.scalar_tensor_tensor(
+                out=scaled[i][:], in0=y[i][:], scalar=negmean[i][:], in1=gamma_ps[:],
+                op0=ALU.add, op1=ALU.mult,
+            )
+
+        def finish_tile(i):
+            result = keep.tile([P, D], F32, name="result%d" % i)
+            nc.vector.scalar_tensor_tensor(
+                out=result[:], in0=scaled[i][:], scalar=rstd[i][:], in1=beta_ps[:],
+                op0=ALU.mult, op1=ALU.add,
+            )
+            nc.sync.dma_start(out=out[0, i * P : (i + 1) * P, :], in_=result[:])
+
+        transpose_tile(0)
+        quantise_tile(0)
+        gamma_ps = spread(gamma_rows, "gamma_ps")
+        beta_ps = spread(beta_rows, "beta_ps")
+        transpose_tile(1)
+        quantise_tile(1)
+        for i in range(ROW_TILES):
+            multiply_tile(i)
+            if i + 2 < ROW_TILES:
+                transpose_tile(i + 2)
+            centre_tile(i)
+            if i + 2 < ROW_TILES:
+                quantise_tile(i + 2)
+            if i >= 1:
+                finish_tile(i - 1)
+        finish_tile(ROW_TILES - 1)

@@ -42,39 +42,45 @@ def tile_heterogeneousgraphtransformer_pb_s_kernel(
         one_col = keep.tile([P, 1], F32)
         nc.vector.memset(bo_rows[:], 0.0)
         nc.vector.memset(w_planes[:].rearrange("p g n -> p (g n)").bitcast(I32), 0)
-        nc.vector.memset(ones[:], 1.0)
-        nc.vector.memset(one_col[:], 1.0)
         nc.vector.memset(gamma_rows[:], 0.0)
         nc.vector.memset(beta_rows[:], 0.0)
-        ident = keep.tile([P, P], F32)
-        make_identity(nc, ident[:])
+        nc.vector.memset(ones[:], 1.0)
+        nc.vector.memset(one_col[:], 1.0)
 
-        nc.sync.dma_start(out=bo_rows[0:1, :], in_=bo.unsqueeze(0))
+        att_sb = [keep.tile([P, E, D], BF16, name="att%d" % i) for i in range(ROW_TILES)]
+        scene_sb = [keep.tile([P, D], BF16, name="scene%d" % i) for i in range(ROW_TILES)]
+        w_words = keep.tile([P, E, 2 * D], U8, align_bytes=64)
+
+        def load_att(i):
+            rows = slice(i * P, (i + 1) * P)
+            nc.sync.dma_start(out=att_sb[i][:], in_=att[:, 0, rows, :].rearrange("e s d -> s e d"))
+
+        def load_scene(i):
+            nc.sync.dma_start(out=scene_sb[i][:], in_=scene_reps[0, i * P : (i + 1) * P, :])
+
+        load_att(0)
         scale_words = Wo_scales.bitcast(I32)
         for r in range(4):
             nc.sync.dma_start(
                 out=w_planes[r:P:32, :, :].bitcast(I32),
                 in_=scale_words[:, r:16:4, :].rearrange("g q w -> q g w"),
             )
+        nc.sync.dma_start(
+            out=w_words[:].bitcast(I32), in_=Wo_words.bitcast(I32).rearrange("g p w -> p g w")
+        )
+        load_att(1)
+        load_att(2)
+        load_scene(0)
+        load_att(3)
+        load_scene(1)
+        load_scene(2)
+        load_scene(3)
+
+        nc.gpsimd.dma_start(out=bo_rows[0:1, :], in_=bo.unsqueeze(0))
+        ident = keep.tile([P, P], F32)
+        make_identity(nc, ident[:])
         nc.gpsimd.dma_start(out=gamma_rows[0:1, :], in_=gamma.unsqueeze(0))
         nc.gpsimd.dma_start(out=beta_rows[0:1, :], in_=beta.unsqueeze(0))
-
-        w_words = keep.tile([P, E, 2 * D], U8, align_bytes=64)
-        att_sb = []
-        scene_sb = []
-        for i in range(ROW_TILES):
-            rows = slice(i * P, (i + 1) * P)
-            att_i = keep.tile([P, E, D], BF16, name="att%d" % i)
-            nc.sync.dma_start(out=att_i[:], in_=att[:, 0, rows, :].rearrange("e s d -> s e d"))
-            att_sb.append(att_i)
-            if i == 0:
-                nc.sync.dma_start(
-                    out=w_words[:].bitcast(I32),
-                    in_=Wo_words.bitcast(I32).rearrange("g p w -> p g w"),
-                )
-            scene_i = keep.tile([P, D], BF16, name="scene%d" % i)
-            nc.sync.dma_start(out=scene_i[:], in_=scene_reps[0, rows, :])
-            scene_sb.append(scene_i)
 
         table_warm = keep.tile([P, 1], F32)
         nc.scalar.activation(out=table_warm[:], in_=one_col[:], func=ACT.Abs_reciprocal_sqrt)
@@ -84,20 +90,11 @@ def tile_heterogeneousgraphtransformer_pb_s_kernel(
             nc.tensor.matmul(out=spread_ps[:], lhsT=ones[:], rhs=rows_tile[:], start=True, stop=True)
             return spread_ps
 
-        bo_ps = spread(bo_rows, "bo_ps")
-        bo_sb = keep.tile([P, D], BF16)
-        nc.scalar.copy(out=bo_sb[:], in_=bo_ps[:])
-
-        resid = []
-        for i in range(ROW_TILES):
-            resid_i = keep.tile([P, D], F32, name="resid%d" % i)
-            nc.gpsimd.tensor_tensor(out=resid_i[:], in0=scene_sb[i][:], in1=bo_sb[:], op=ALU.add)
-            resid.append(resid_i)
-
         grouped = {}
         codes = {}
         planes = {}
         acc = {}
+        resid = {}
         y = {}
         negmean = {}
         rstd = {}
@@ -134,6 +131,10 @@ def tile_heterogeneousgraphtransformer_pb_s_kernel(
                     stop=(g == E - 1),
                 )
 
+        def add_bias_to_residual(i):
+            resid[i] = keep.tile([P, D], F32, name="resid%d" % i)
+            nc.gpsimd.tensor_tensor(out=resid[i][:], in0=scene_sb[i][:], in1=bo_sb[:], op=ALU.add)
+
         def centre_tile(i):
             y[i] = keep.tile([P, D], F32, name="y%d" % i)
             y_sum = keep.tile([P, 1], F32, name="ysum%d" % i)
@@ -163,25 +164,44 @@ def tile_heterogeneousgraphtransformer_pb_s_kernel(
 
         def finish_tile(i):
             result = keep.tile([P, D], F32, name="result%d" % i)
-            nc.vector.scalar_tensor_tensor(
-                out=result[:], in0=scaled[i][:], scalar=rstd[i][:], in1=beta_ps[:],
-                op0=ALU.mult, op1=ALU.add,
-            )
+            if i < ROW_TILES - 1:
+                normed = keep.tile([P, D], F32, name="normed%d" % i)
+                nc.scalar.activation(out=normed[:], in_=scaled[i][:], func=ACT.Copy, scale=rstd[i][:])
+                nc.gpsimd.tensor_tensor(out=result[:], in0=normed[:], in1=beta_sb[:], op=ALU.add)
+            else:
+                nc.vector.scalar_tensor_tensor(
+                    out=result[:], in0=scaled[i][:], scalar=rstd[i][:], in1=beta_ps[:],
+                    op0=ALU.mult, op1=ALU.add,
+                )
             nc.sync.dma_start(out=out[0, i * P : (i + 1) * P, :], in_=result[:])
 
         transpose_tile(0)
+        bo_ps = spread(bo_rows, "bo_ps")
+        bo_sb = keep.tile([P, D], BF16)
+        nc.scalar.copy(out=bo_sb[:], in_=bo_ps[:])
         quantise_tile(0)
-        gamma_ps = spread(gamma_rows, "gamma_ps")
-        beta_ps = spread(beta_rows, "beta_ps")
         transpose_tile(1)
         quantise_tile(1)
         for i in range(ROW_TILES):
+            add_bias_to_residual(i)
+
+        multiply_tile(0)
+        gamma_ps = spread(gamma_rows, "gamma_ps")
+        transpose_tile(2)
+        beta_ps = spread(beta_rows, "beta_ps")
+        centre_tile(0)
+        quantise_tile(2)
+        beta_sb = keep.tile([P, D], BF16)
+        nc.scalar.copy(out=beta_sb[:], in_=beta_ps[:])
+        finish_tile(0)
+
+        multiply_tile(1)
+        transpose_tile(3)
+        centre_tile(1)
+        quantise_tile(3)
+        finish_tile(1)
+
+        for i in range(2, ROW_TILES):
             multiply_tile(i)
-            if i + 2 < ROW_TILES:
-                transpose_tile(i + 2)
             centre_tile(i)
-            if i + 2 < ROW_TILES:
-                quantise_tile(i + 2)
-            if i >= 1:
-                finish_tile(i - 1)
-        finish_tile(ROW_TILES - 1)
+            finish_tile(i)

@@ -34,14 +34,14 @@ def tile_heterogeneousgraphtransformer_pb_s_kernel(
         psum_acc = ctx.enter_context(tc.psum_pool(name="psum_acc", bufs=3))
         ctx.enter_context(tc.manual_schedule())
 
-        bo_rows = keep.tile([P, D], BF16)
         w_planes = keep.tile([P, E, D], U8, align_bytes=64)
+        bo_rows = keep.tile([P, D], BF16)
         gamma_rows = keep.tile([P, D], BF16)
         beta_rows = keep.tile([P, D], BF16)
         ones = keep.tile([P, P], BF16)
         one_col = keep.tile([P, 1], F32)
-        nc.vector.memset(bo_rows[:], 0.0)
         nc.vector.memset(w_planes[:].rearrange("p g n -> p (g n)").bitcast(I32), 0)
+        nc.vector.memset(bo_rows[:], 0.0)
         nc.vector.memset(gamma_rows[:], 0.0)
         nc.vector.memset(beta_rows[:], 0.0)
         nc.vector.memset(ones[:], 1.0)
@@ -65,18 +65,18 @@ def tile_heterogeneousgraphtransformer_pb_s_kernel(
                 out=w_planes[r:P:32, :, :].bitcast(I32),
                 in_=scale_words[:, r:16:4, :].rearrange("g q w -> q g w"),
             )
+        load_att(1)
         nc.sync.dma_start(
             out=w_words[:].bitcast(I32), in_=Wo_words.bitcast(I32).rearrange("g p w -> p g w")
         )
-        load_att(1)
-        load_att(2)
+        nc.sync.dma_start(out=bo_rows[0:1, :], in_=bo.unsqueeze(0))
         load_scene(0)
+        load_att(2)
         load_att(3)
         load_scene(1)
         load_scene(2)
         load_scene(3)
 
-        nc.gpsimd.dma_start(out=bo_rows[0:1, :], in_=bo.unsqueeze(0))
         ident = keep.tile([P, P], F32)
         make_identity(nc, ident[:])
         nc.gpsimd.dma_start(out=gamma_rows[0:1, :], in_=gamma.unsqueeze(0))
@@ -131,10 +131,6 @@ def tile_heterogeneousgraphtransformer_pb_s_kernel(
                     stop=(g == E - 1),
                 )
 
-        def add_bias_to_residual(i):
-            resid[i] = keep.tile([P, D], F32, name="resid%d" % i)
-            nc.gpsimd.tensor_tensor(out=resid[i][:], in0=scene_sb[i][:], in1=bo_sb[:], op=ALU.add)
-
         def centre_tile(i):
             y[i] = keep.tile([P, D], F32, name="y%d" % i)
             y_sum = keep.tile([P, 1], F32, name="ysum%d" % i)
@@ -162,46 +158,53 @@ def tile_heterogeneousgraphtransformer_pb_s_kernel(
                 op0=ALU.add, op1=ALU.mult,
             )
 
-        def finish_tile(i):
+        def finish_on_scalar_and_gpsimd(i):
+            normed = keep.tile([P, D], F32, name="normed%d" % i)
+            nc.scalar.activation(out=normed[:], in_=scaled[i][:], func=ACT.Copy, scale=rstd[i][:])
             result = keep.tile([P, D], F32, name="result%d" % i)
-            if i < ROW_TILES - 1:
-                normed = keep.tile([P, D], F32, name="normed%d" % i)
-                nc.scalar.activation(out=normed[:], in_=scaled[i][:], func=ACT.Copy, scale=rstd[i][:])
-                nc.gpsimd.tensor_tensor(out=result[:], in0=normed[:], in1=beta_sb[:], op=ALU.add)
-            else:
-                nc.vector.scalar_tensor_tensor(
-                    out=result[:], in0=scaled[i][:], scalar=rstd[i][:], in1=beta_ps[:],
-                    op0=ALU.mult, op1=ALU.add,
-                )
+            nc.gpsimd.tensor_tensor(out=result[:], in0=normed[:], in1=beta_sb[:], op=ALU.add)
+            nc.sync.dma_start(out=out[0, i * P : (i + 1) * P, :], in_=result[:])
+
+        def finish_on_vector(i):
+            result = keep.tile([P, D], F32, name="result%d" % i)
+            nc.vector.scalar_tensor_tensor(
+                out=result[:], in0=scaled[i][:], scalar=rstd[i][:], in1=beta_ps[:],
+                op0=ALU.mult, op1=ALU.add,
+            )
             nc.sync.dma_start(out=out[0, i * P : (i + 1) * P, :], in_=result[:])
 
         transpose_tile(0)
+        transpose_tile(1)
         bo_ps = spread(bo_rows, "bo_ps")
+        quantise_tile(0)
+        resid[0] = keep.tile([P, D], F32, name="resid0")
+        nc.vector.tensor_tensor(out=resid[0][:], in0=scene_sb[0][:], in1=bo_ps[:], op=ALU.add)
         bo_sb = keep.tile([P, D], BF16)
         nc.scalar.copy(out=bo_sb[:], in_=bo_ps[:])
-        quantise_tile(0)
-        transpose_tile(1)
         quantise_tile(1)
-        for i in range(ROW_TILES):
-            add_bias_to_residual(i)
-
+        for i in range(1, ROW_TILES):
+            resid[i] = keep.tile([P, D], F32, name="resid%d" % i)
+            nc.gpsimd.tensor_tensor(out=resid[i][:], in0=scene_sb[i][:], in1=bo_sb[:], op=ALU.add)
         multiply_tile(0)
         gamma_ps = spread(gamma_rows, "gamma_ps")
         transpose_tile(2)
-        beta_ps = spread(beta_rows, "beta_ps")
+        multiply_tile(1)
+
         centre_tile(0)
         quantise_tile(2)
+        transpose_tile(3)
+        beta_ps = spread(beta_rows, "beta_ps")
         beta_sb = keep.tile([P, D], BF16)
         nc.scalar.copy(out=beta_sb[:], in_=beta_ps[:])
-        finish_tile(0)
+        multiply_tile(2)
+        finish_on_scalar_and_gpsimd(0)
 
-        multiply_tile(1)
-        transpose_tile(3)
         centre_tile(1)
         quantise_tile(3)
-        finish_tile(1)
+        multiply_tile(3)
+        finish_on_scalar_and_gpsimd(1)
 
-        for i in range(2, ROW_TILES):
-            multiply_tile(i)
-            centre_tile(i)
-            finish_tile(i)
+        centre_tile(2)
+        centre_tile(3)
+        finish_on_vector(2)
+        finish_on_vector(3)

@@ -37,13 +37,13 @@ def tile_heterogeneousgraphtransformer_pb_s_kernel(
         w_planes = keep.tile([P, E, D], U8, align_bytes=64)
         bo_rows = keep.tile([P, D], BF16)
         gamma_rows = keep.tile([P, D], BF16)
-        beta_rows = keep.tile([P, D], BF16)
         ones = keep.tile([P, P], BF16)
         one_col = keep.tile([P, 1], F32)
+        warm_in = keep.tile([P, P], F32)
+        nc.vector.memset(warm_in[:], 0.0)
         nc.vector.memset(w_planes[:].rearrange("p g n -> p (g n)").bitcast(I32), 0)
         nc.vector.memset(bo_rows[:], 0.0)
         nc.vector.memset(gamma_rows[:], 0.0)
-        nc.vector.memset(beta_rows[:], 0.0)
         nc.vector.memset(ones[:], 1.0)
         nc.vector.memset(one_col[:], 1.0)
 
@@ -76,11 +76,12 @@ def tile_heterogeneousgraphtransformer_pb_s_kernel(
         load_scene(1)
         load_scene(2)
         load_scene(3)
+        beta_sb = keep.tile([P, D], BF16)
+        nc.sync.dma_start(out=beta_sb[:], in_=beta.partition_broadcast(P))
 
         ident = keep.tile([P, P], F32)
         make_identity(nc, ident[:])
         nc.gpsimd.dma_start(out=gamma_rows[0:1, :], in_=gamma.unsqueeze(0))
-        nc.gpsimd.dma_start(out=beta_rows[0:1, :], in_=beta.unsqueeze(0))
 
         table_warm = keep.tile([P, 1], F32)
         nc.scalar.activation(out=table_warm[:], in_=one_col[:], func=ACT.Abs_reciprocal_sqrt)
@@ -89,6 +90,10 @@ def tile_heterogeneousgraphtransformer_pb_s_kernel(
             spread_ps = psum_rows.tile([P, D], F32, name=name)
             nc.tensor.matmul(out=spread_ps[:], lhsT=ones[:], rhs=rows_tile[:], start=True, stop=True)
             return spread_ps
+
+        warm_ps = psum_rows.tile([P, P], F32, name="warm_ps")
+        for j in range(4):
+            nc.tensor.matmul(out=warm_ps[:], lhsT=warm_in[:], rhs=warm_in[:], start=True, stop=True)
 
         grouped = {}
         codes = {}
@@ -168,7 +173,7 @@ def tile_heterogeneousgraphtransformer_pb_s_kernel(
         def finish_on_vector(i):
             result = keep.tile([P, D], F32, name="result%d" % i)
             nc.vector.scalar_tensor_tensor(
-                out=result[:], in0=scaled[i][:], scalar=rstd[i][:], in1=beta_ps[:],
+                out=result[:], in0=scaled[i][:], scalar=rstd[i][:], in1=beta_sb[:],
                 op0=ALU.mult, op1=ALU.add,
             )
             nc.sync.dma_start(out=out[0, i * P : (i + 1) * P, :], in_=result[:])
@@ -193,9 +198,6 @@ def tile_heterogeneousgraphtransformer_pb_s_kernel(
         centre_tile(0)
         quantise_tile(2)
         transpose_tile(3)
-        beta_ps = spread(beta_rows, "beta_ps")
-        beta_sb = keep.tile([P, D], BF16)
-        nc.scalar.copy(out=beta_sb[:], in_=beta_ps[:])
         multiply_tile(2)
         finish_on_scalar_and_gpsimd(0)
 

@@ -91,9 +91,21 @@ def tile_heterogeneousgraphtransformer_pb_s_kernel(
             nc.tensor.matmul(out=spread_ps[:], lhsT=ones[:], rhs=rows_tile[:], start=True, stop=True)
             return spread_ps
 
-        warm_ps = psum_rows.tile([P, P], F32, name="warm_ps")
+        warm_ps = psum_rows.tile([P, D], F32, name="warm_ps")
         for j in range(4):
-            nc.tensor.matmul(out=warm_ps[:], lhsT=warm_in[:], rhs=warm_in[:], start=True, stop=True)
+            nc.tensor.matmul(out=warm_ps[:, 0:P], lhsT=warm_in[:], rhs=warm_in[:], start=True, stop=True)
+
+        def dummy_pass(i):
+            cols = slice((E - 1) * P, E * P)
+            nc.tensor.matmul_mx(
+                out=warm_ps[:],
+                lhsT=codes[i][:, cols].bitcast(FP8X4),
+                lhsT_scale=planes[i][:, cols],
+                rhs=w_words[:, E - 1, :].bitcast(FP4X4),
+                rhs_scale=w_planes[:, E - 1, :],
+                start=True,
+                stop=True,
+            )
 
         grouped = {}
         codes = {}
@@ -191,14 +203,17 @@ def tile_heterogeneousgraphtransformer_pb_s_kernel(
             resid[i] = keep.tile([P, D], F32, name="resid%d" % i)
             nc.gpsimd.tensor_tensor(out=resid[i][:], in0=scene_sb[i][:], in1=bo_sb[:], op=ALU.add)
         multiply_tile(0)
+        dummy_pass(0)
         gamma_ps = spread(gamma_rows, "gamma_ps")
         transpose_tile(2)
         multiply_tile(1)
+        dummy_pass(1)
 
         centre_tile(0)
         quantise_tile(2)
         transpose_tile(3)
         multiply_tile(2)
+        dummy_pass(2)
         finish_on_scalar_and_gpsimd(0)
 
         centre_tile(1)

@@ -40,42 +40,46 @@ def tile_heterogeneousgraphtransformer_pb_s_kernel(
         ones = keep.tile([P, P], BF16)
         one_col = keep.tile([P, 1], F32)
         warm_in = keep.tile([P, P], F32)
+        nc.vector.memset(bo_rows[:].bitcast(I32), 0)
         nc.vector.memset(warm_in[:], 0.0)
         nc.vector.memset(w_planes[:].rearrange("p g n -> p (g n)").bitcast(I32), 0)
-        nc.vector.memset(bo_rows[:], 0.0)
-        nc.vector.memset(gamma_rows[:], 0.0)
         nc.vector.memset(ones[:], 1.0)
         nc.vector.memset(one_col[:], 1.0)
+        nc.vector.memset(gamma_rows[:].bitcast(I32), 0)
 
-        att_sb = [keep.tile([P, E, D], BF16, name="att%d" % i) for i in range(ROW_TILES)]
-        scene_sb = [keep.tile([P, D], BF16, name="scene%d" % i) for i in range(ROW_TILES)]
+        att_blocks = att[:, 0, :, :].rearrange("e (i s) d -> s (e i) d", s=P)
+        scene_blocks = scene_reps[0, :, :].rearrange("(i s) d -> s i d", s=P)
+        att_one = {i: keep.tile([P, E, D], BF16, name="att%d" % i) for i in (0, 2)}
+        att_pair = keep.tile([P, E, 2, D], BF16)
+        scene_even = keep.tile([P, 2, D], BF16)
+        scene_odd = keep.tile([P, 2, D], BF16)
         w_words = keep.tile([P, E, 2 * D], U8, align_bytes=64)
 
-        def load_att(i):
-            rows = slice(i * P, (i + 1) * P)
-            nc.sync.dma_start(out=att_sb[i][:], in_=att[:, 0, rows, :].rearrange("e s d -> s e d"))
+        def att_view(i, g):
+            if i in att_one:
+                return att_one[i][:, g, :]
+            return att_pair[:, g, i // 2, :]
 
-        def load_scene(i):
-            nc.sync.dma_start(out=scene_sb[i][:], in_=scene_reps[0, i * P : (i + 1) * P, :])
+        def scene_view(i):
+            return (scene_odd if i % 2 else scene_even)[:, i // 2, :]
 
-        load_att(0)
+        nc.sync.dma_start(out=att_one[0][:], in_=att_blocks[:, 0 : 2 * ROW_TILES : ROW_TILES, :])
+        nc.sync.dma_start(out=bo_rows[0:1, :], in_=bo.unsqueeze(0))
+        nc.sync.dma_start(out=scene_even[:], in_=scene_blocks[:, 0:ROW_TILES:2, :])
+        nc.sync.dma_start(out=att_one[2][:], in_=att_blocks[:, 2 : 2 * ROW_TILES : ROW_TILES, :])
+        nc.sync.dma_start(
+            out=w_words[:].bitcast(I32), in_=Wo_words.bitcast(I32).rearrange("g p w -> p g w")
+        )
         scale_words = Wo_scales.bitcast(I32)
         for r in range(4):
             nc.sync.dma_start(
                 out=w_planes[r:P:32, :, :].bitcast(I32),
                 in_=scale_words[:, r:16:4, :].rearrange("g q w -> q g w"),
             )
-        load_att(1)
         nc.sync.dma_start(
-            out=w_words[:].bitcast(I32), in_=Wo_words.bitcast(I32).rearrange("g p w -> p g w")
+            out=att_pair[:].rearrange("p e i d -> p (e i) d"), in_=att_blocks[:, 1 : 2 * ROW_TILES : 2, :]
         )
-        nc.sync.dma_start(out=bo_rows[0:1, :], in_=bo.unsqueeze(0))
-        load_scene(0)
-        load_att(2)
-        load_att(3)
-        load_scene(1)
-        load_scene(2)
-        load_scene(3)
+        nc.sync.dma_start(out=scene_odd[:], in_=scene_blocks[:, 1:ROW_TILES:2, :])
         beta_sb = keep.tile([P, D], BF16)
         nc.sync.dma_start(out=beta_sb[:], in_=beta.partition_broadcast(P))
 
@@ -92,49 +96,43 @@ def tile_heterogeneousgraphtransformer_pb_s_kernel(
             return spread_ps
 
         warm_ps = psum_rows.tile([P, D], F32, name="warm_ps")
-        for j in range(4):
-            nc.tensor.matmul(out=warm_ps[:, 0:P], lhsT=warm_in[:], rhs=warm_in[:], start=True, stop=True)
 
-        def dummy_pass(i):
-            cols = slice((E - 1) * P, E * P)
-            nc.tensor.matmul_mx(
-                out=warm_ps[:],
-                lhsT=codes[i][:, cols].bitcast(FP8X4),
-                lhsT_scale=planes[i][:, cols],
-                rhs=w_words[:, E - 1, :].bitcast(FP4X4),
-                rhs_scale=w_planes[:, E - 1, :],
-                start=True,
-                stop=True,
-            )
+        def dummies(count):
+            for j in range(count):
+                nc.tensor.matmul(out=warm_ps[:, 0:P], lhsT=warm_in[:], rhs=warm_in[:], start=True, stop=True)
 
+        xts = {}
         grouped = {}
         codes = {}
         planes = {}
         acc = {}
         resid = {}
         y = {}
+        y_sum = {}
         negmean = {}
         rstd = {}
         scaled = {}
 
-        def transpose_tile(i):
-            xt = psum_xt.tile([P, E, 2, P], F32, name="xt")
+        def transpose(i):
+            xts[i] = psum_xt.tile([P, E, 2, P], F32, name="xt")
             for g in range(E):
-                words = att_sb[i][:, g, :].bitcast(F32)
+                words = att_view(i, g).bitcast(F32)
                 for u in range(2):
-                    nc.tensor.transpose(xt[:, g, u, :], words[:, u : D // 2 : 2], ident[:])
+                    nc.tensor.transpose(xts[i][:, g, u, :], words[:, u : D // 2 : 2], ident[:])
+
+        def regroup(i):
             grouped[i] = keep.tile([P, E * P * 4], BF16, name="grouped%d" % i, align_bytes=64)
             nc.scalar.copy(
                 out=grouped[i][:].bitcast(F32).rearrange("p (g s u) -> p g s u", g=E, u=2),
-                in_=xt[:].rearrange("p g u s -> p g s u"),
+                in_=xts[i][:].rearrange("p g u s -> p g s u"),
             )
 
-        def quantise_tile(i):
+        def quantise(i):
             codes[i] = keep.tile([P, E * P], U32, name="codes%d" % i, align_bytes=64)
             planes[i] = keep.tile([P, E * P], U8, name="planes%d" % i, align_bytes=64)
             nc.vector.quantize_mx(out=codes[i][:].bitcast(FP8X4), scales=planes[i][:], in_=grouped[i][:])
 
-        def multiply_tile(i):
+        def multiply(i):
             acc[i] = psum_acc.tile([P, D], F32, name="acc")
             for g in range(E):
                 cols = slice(g * P, (g + 1) * P)
@@ -148,39 +146,53 @@ def tile_heterogeneousgraphtransformer_pb_s_kernel(
                     stop=(g == E - 1),
                 )
 
-        def centre_tile(i):
+        def residual_on_vector(i):
+            resid[i] = keep.tile([P, D], F32, name="resid%d" % i)
+            nc.vector.tensor_tensor(out=resid[i][:], in0=scene_view(i), in1=bo_ps[:], op=ALU.add)
+
+        def residual_on_gpsimd(i):
+            resid[i] = keep.tile([P, D], F32, name="resid%d" % i)
+            nc.gpsimd.tensor_tensor(out=resid[i][:], in0=scene_view(i), in1=bo_sb[:], op=ALU.add)
+
+        def add_residual(i):
             y[i] = keep.tile([P, D], F32, name="y%d" % i)
-            y_sum = keep.tile([P, 1], F32, name="ysum%d" % i)
+            y_sum[i] = keep.tile([P, 1], F32, name="ysum%d" % i)
             nc.vector.scalar_tensor_tensor(
                 out=y[i][:], in0=acc[i][:], scalar=1.0, in1=resid[i][:],
-                op0=ALU.mult, op1=ALU.add, accum_out=y_sum[:],
+                op0=ALU.mult, op1=ALU.add, accum_out=y_sum[i][:],
             )
+
+        def negative_mean(i):
             negmean[i] = keep.tile([P, 1], F32, name="negmean%d" % i)
-            nc.vector.tensor_scalar(
-                out=negmean[i][:], in0=y_sum[:], scalar1=-1.0 / D, scalar2=None, op0=ALU.mult
-            )
+            nc.scalar.activation(out=negmean[i][:], in_=y_sum[i][:], func=ACT.Copy, scale=-1.0 / D)
+        def moments(i):
             squares = keep.tile([P, D], F32, name="squares%d" % i)
             sq_sum = keep.tile([P, 1], F32, name="sqsum%d" % i)
             nc.scalar.activation(
-                out=squares[:], in_=y[i][:], func=ACT.Square, bias=negmean[i][:], scale=1.0,
+                out=squares[:], in_=y[i][:], func=ACT.Square, bias=y_sum[i][:], scale=-float(D),
                 accum_out=sq_sum[:],
             )
             rstd[i] = keep.tile([P, 1], F32, name="rstd%d" % i)
             nc.scalar.activation(
-                out=rstd[i][:], in_=sq_sum[:], func=ACT.Abs_reciprocal_sqrt, bias=EPS, scale=1.0 / D
+                out=rstd[i][:], in_=sq_sum[:], func=ACT.Abs_reciprocal_sqrt, bias=EPS, scale=1.0 / D**3
             )
+
+        def centre_and_gamma(i):
             scaled[i] = keep.tile([P, D], F32, name="scaled%d" % i)
             nc.vector.scalar_tensor_tensor(
                 out=scaled[i][:], in0=y[i][:], scalar=negmean[i][:], in1=gamma_ps[:],
                 op0=ALU.add, op1=ALU.mult,
             )
 
+        def store(i, result):
+            nc.sync.dma_start(out=out[0, i * P : (i + 1) * P, :], in_=result[:])
+
         def finish_on_scalar_and_gpsimd(i):
             normed = keep.tile([P, D], F32, name="normed%d" % i)
             nc.scalar.activation(out=normed[:], in_=scaled[i][:], func=ACT.Copy, scale=rstd[i][:])
             result = keep.tile([P, D], F32, name="result%d" % i)
             nc.gpsimd.tensor_tensor(out=result[:], in0=normed[:], in1=beta_sb[:], op=ALU.add)
-            nc.sync.dma_start(out=out[0, i * P : (i + 1) * P, :], in_=result[:])
+            store(i, result)
 
         def finish_on_vector(i):
             result = keep.tile([P, D], F32, name="result%d" % i)
@@ -188,40 +200,52 @@ def tile_heterogeneousgraphtransformer_pb_s_kernel(
                 out=result[:], in0=scaled[i][:], scalar=rstd[i][:], in1=beta_sb[:],
                 op0=ALU.mult, op1=ALU.add,
             )
-            nc.sync.dma_start(out=out[0, i * P : (i + 1) * P, :], in_=result[:])
+            store(i, result)
 
-        transpose_tile(0)
-        transpose_tile(1)
+        dummies(2)
         bo_ps = spread(bo_rows, "bo_ps")
-        quantise_tile(0)
-        resid[0] = keep.tile([P, D], F32, name="resid0")
-        nc.vector.tensor_tensor(out=resid[0][:], in0=scene_sb[0][:], in1=bo_ps[:], op=ALU.add)
+        residual_on_vector(0)
+        residual_on_vector(2)
+        transpose(0)
+        transpose(2)
+        dummies(2)
+        regroup(0)
+        regroup(2)
         bo_sb = keep.tile([P, D], BF16)
         nc.scalar.copy(out=bo_sb[:], in_=bo_ps[:])
-        quantise_tile(1)
-        for i in range(1, ROW_TILES):
-            resid[i] = keep.tile([P, D], F32, name="resid%d" % i)
-            nc.gpsimd.tensor_tensor(out=resid[i][:], in0=scene_sb[i][:], in1=bo_sb[:], op=ALU.add)
-        multiply_tile(0)
-        dummy_pass(0)
+        quantise(0)
+        quantise(2)
+        multiply(0)
+        multiply(2)
+        transpose(1)
         gamma_ps = spread(gamma_rows, "gamma_ps")
-        transpose_tile(2)
-        multiply_tile(1)
-        dummy_pass(1)
+        transpose(3)
+        residual_on_gpsimd(1)
+        residual_on_gpsimd(3)
 
-        centre_tile(0)
-        quantise_tile(2)
-        transpose_tile(3)
-        multiply_tile(2)
-        dummy_pass(2)
+        add_residual(0)
+        add_residual(2)
+        negative_mean(0)
+        regroup(1)
+        regroup(3)
+        centre_and_gamma(0)
+        quantise(1)
+        quantise(3)
+        multiply(1)
+        multiply(3)
+        moments(0)
+        negative_mean(2)
+        moments(2)
+        centre_and_gamma(2)
+        add_residual(1)
         finish_on_scalar_and_gpsimd(0)
-
-        centre_tile(1)
-        quantise_tile(3)
-        multiply_tile(3)
-        finish_on_scalar_and_gpsimd(1)
-
-        centre_tile(2)
-        centre_tile(3)
-        finish_on_vector(2)
+        negative_mean(1)
+        moments(1)
+        finish_on_scalar_and_gpsimd(2)
+        add_residual(3)
+        negative_mean(3)
+        moments(3)
+        centre_and_gamma(1)
+        centre_and_gamma(3)
+        finish_on_vector(1)
         finish_on_vector(3)

@@ -151,7 +151,7 @@ def tile_heterogeneousgraphtransformer_pb_s_kernel(
             nc.vector.tensor_tensor(out=resid[i][:], in0=scene_view(i), in1=bo_ps[:], op=ALU.add)
 
         def residual_on_gpsimd(i):
-            resid[i] = keep.tile([P, D], F32, name="resid%d" % i)
+            resid[i] = keep.tile([P, D], F32, name="grouped3" if i == 3 else "resid%d" % i, align_bytes=64)
             nc.gpsimd.tensor_tensor(out=resid[i][:], in0=scene_view(i), in1=bo_sb[:], op=ALU.add)
 
         def add_residual(i):
@@ -221,7 +221,6 @@ def tile_heterogeneousgraphtransformer_pb_s_kernel(
         gamma_ps = spread(gamma_rows, "gamma_ps")
         transpose(3)
         residual_on_gpsimd(1)
-        residual_on_gpsimd(3)
 
         add_residual(0)
         add_residual(2)
@@ -231,6 +230,7 @@ def tile_heterogeneousgraphtransformer_pb_s_kernel(
         centre_and_gamma(0)
         quantise(1)
         quantise(3)
+        residual_on_gpsimd(3)
         multiply(1)
         multiply(3)
         moments(0)
@@ -239,9 +239,9 @@ def tile_heterogeneousgraphtransformer_pb_s_kernel(
         centre_and_gamma(2)
         add_residual(1)
         finish_on_scalar_and_gpsimd(0)
+        finish_on_scalar_and_gpsimd(2)
         negative_mean(1)
         moments(1)
-        finish_on_scalar_and_gpsimd(2)
         add_residual(3)
         negative_mean(3)
         moments(3)

@@ -151,7 +151,7 @@ def tile_heterogeneousgraphtransformer_pb_s_kernel(
             nc.vector.tensor_tensor(out=resid[i][:], in0=scene_view(i), in1=bo_ps[:], op=ALU.add)
 
         def residual_on_gpsimd(i):
-            resid[i] = keep.tile([P, D], F32, name="grouped3" if i == 3 else "resid%d" % i, align_bytes=64)
+            resid[i] = keep.tile([P, D], F32, name="grouped%d" % {1: 2, 3: 3}[i], align_bytes=64)
             nc.gpsimd.tensor_tensor(out=resid[i][:], in0=scene_view(i), in1=bo_sb[:], op=ALU.add)
 
         def add_residual(i):

@@ -109,6 +109,7 @@ def tile_heterogeneousgraphtransformer_pb_s_kernel(
         resid = {}
         y = {}
         y_sum = {}
+        sq_sum = {}
         negmean = {}
         rstd = {}
         scaled = {}
@@ -165,16 +166,19 @@ def tile_heterogeneousgraphtransformer_pb_s_kernel(
         def negative_mean(i):
             negmean[i] = keep.tile([P, 1], F32, name="negmean%d" % i)
             nc.scalar.activation(out=negmean[i][:], in_=y_sum[i][:], func=ACT.Copy, scale=-1.0 / D)
-        def moments(i):
+
+        def squares_of(i):
             squares = keep.tile([P, D], F32, name="squares%d" % i)
-            sq_sum = keep.tile([P, 1], F32, name="sqsum%d" % i)
+            sq_sum[i] = keep.tile([P, 1], F32, name="sqsum%d" % i)
             nc.scalar.activation(
                 out=squares[:], in_=y[i][:], func=ACT.Square, bias=y_sum[i][:], scale=-float(D),
-                accum_out=sq_sum[:],
+                accum_out=sq_sum[i][:],
             )
+
+        def reciprocal_std(i):
             rstd[i] = keep.tile([P, 1], F32, name="rstd%d" % i)
             nc.scalar.activation(
-                out=rstd[i][:], in_=sq_sum[:], func=ACT.Abs_reciprocal_sqrt, bias=EPS, scale=1.0 / D**3
+                out=rstd[i][:], in_=sq_sum[i][:], func=ACT.Abs_reciprocal_sqrt, bias=EPS, scale=1.0 / D**3
             )
 
         def centre_and_gamma(i):
@@ -184,15 +188,15 @@ def tile_heterogeneousgraphtransformer_pb_s_kernel(
                 op0=ALU.add, op1=ALU.mult,
             )
 
-        def store(i, result):
-            nc.sync.dma_start(out=out[0, i * P : (i + 1) * P, :], in_=result[:])
+        def store(queue, i, result):
+            queue.dma_start(out=out[0, i * P : (i + 1) * P, :], in_=result[:])
 
         def finish_on_scalar_and_gpsimd(i):
             normed = keep.tile([P, D], F32, name="normed%d" % i)
             nc.scalar.activation(out=normed[:], in_=scaled[i][:], func=ACT.Copy, scale=rstd[i][:])
             result = keep.tile([P, D], F32, name="result%d" % i)
             nc.gpsimd.tensor_tensor(out=result[:], in0=normed[:], in1=beta_sb[:], op=ALU.add)
-            store(i, result)
+            store(nc.sync, i, result)
 
         def finish_on_vector(i):
             result = keep.tile([P, D], F32, name="result%d" % i)
@@ -200,7 +204,7 @@ def tile_heterogeneousgraphtransformer_pb_s_kernel(
                 out=result[:], in0=scaled[i][:], scalar=rstd[i][:], in1=beta_sb[:],
                 op0=ALU.mult, op1=ALU.add,
             )
-            store(i, result)
+            store(nc.sync, i, result)
 
         dummies(2)
         bo_ps = spread(bo_rows, "bo_ps")
@@ -216,35 +220,39 @@ def tile_heterogeneousgraphtransformer_pb_s_kernel(
         quantise(0)
         quantise(2)
         multiply(0)
-        multiply(2)
         transpose(1)
+        multiply(2)
         gamma_ps = spread(gamma_rows, "gamma_ps")
         transpose(3)
         residual_on_gpsimd(1)
 
         add_residual(0)
-        add_residual(2)
-        negative_mean(0)
         regroup(1)
+        negative_mean(0)
+        squares_of(0)
         regroup(3)
-        centre_and_gamma(0)
+        add_residual(2)
         quantise(1)
+        centre_and_gamma(0)
         quantise(3)
         residual_on_gpsimd(3)
         multiply(1)
         multiply(3)
-        moments(0)
         negative_mean(2)
-        moments(2)
+        squares_of(2)
         centre_and_gamma(2)
         add_residual(1)
+        reciprocal_std(0)
         finish_on_scalar_and_gpsimd(0)
-        finish_on_scalar_and_gpsimd(2)
         negative_mean(1)
-        moments(1)
+        reciprocal_std(2)
+        finish_on_scalar_and_gpsimd(2)
+        squares_of(1)
         add_residual(3)
         negative_mean(3)
-        moments(3)
+        reciprocal_std(1)
+        squares_of(3)
+        reciprocal_std(3)
         centre_and_gamma(1)
         centre_and_gamma(3)
         finish_on_vector(1)

@@ -49,24 +49,21 @@ def tile_heterogeneousgraphtransformer_pb_s_kernel(
 
         att_blocks = att[:, 0, :, :].rearrange("e (i s) d -> s (e i) d", s=P)
         scene_blocks = scene_reps[0, :, :].rearrange("(i s) d -> s i d", s=P)
-        att_one = {i: keep.tile([P, E, D], BF16, name="att%d" % i) for i in (0, 2)}
-        att_pair = keep.tile([P, E, 2, D], BF16)
+        att_sb = [keep.tile([P, E, D], BF16, name="att%d" % i) for i in range(ROW_TILES)]
         scene_even = keep.tile([P, 2, D], BF16)
         scene_odd = keep.tile([P, 2, D], BF16)
         w_words = keep.tile([P, E, 2 * D], U8, align_bytes=64)
 
-        def att_view(i, g):
-            if i in att_one:
-                return att_one[i][:, g, :]
-            return att_pair[:, g, i // 2, :]
+        def load_att(i):
+            nc.sync.dma_start(out=att_sb[i][:], in_=att_blocks[:, i : E * ROW_TILES : ROW_TILES, :])
 
         def scene_view(i):
             return (scene_odd if i % 2 else scene_even)[:, i // 2, :]
 
-        nc.sync.dma_start(out=att_one[0][:], in_=att_blocks[:, 0 : 2 * ROW_TILES : ROW_TILES, :])
+        load_att(0)
         nc.sync.dma_start(out=bo_rows[0:1, :], in_=bo.unsqueeze(0))
         nc.sync.dma_start(out=scene_even[:], in_=scene_blocks[:, 0:ROW_TILES:2, :])
-        nc.sync.dma_start(out=att_one[2][:], in_=att_blocks[:, 2 : 2 * ROW_TILES : ROW_TILES, :])
+        load_att(2)
         nc.sync.dma_start(
             out=w_words[:].bitcast(I32), in_=Wo_words.bitcast(I32).rearrange("g p w -> p g w")
         )
@@ -76,9 +73,8 @@ def tile_heterogeneousgraphtransformer_pb_s_kernel(
                 out=w_planes[r:P:32, :, :].bitcast(I32),
                 in_=scale_words[:, r:16:4, :].rearrange("g q w -> q g w"),
             )
-        nc.sync.dma_start(
-            out=att_pair[:].rearrange("p e i d -> p (e i) d"), in_=att_blocks[:, 1 : 2 * ROW_TILES : 2, :]
-        )
+        load_att(1)
+        load_att(3)
         nc.sync.dma_start(out=scene_odd[:], in_=scene_blocks[:, 1:ROW_TILES:2, :])
         beta_sb = keep.tile([P, D], BF16)
         nc.sync.dma_start(out=beta_sb[:], in_=beta.partition_broadcast(P))
@@ -117,7 +113,7 @@ def tile_heterogeneousgraphtransformer_pb_s_kernel(
         def transpose(i):
             xts[i] = psum_xt.tile([P, E, 2, P], F32, name="xt")
             for g in range(E):
-                words = att_view(i, g).bitcast(F32)
+                words = att_sb[i][:, g, :].bitcast(F32)
                 for u in range(2):
                     nc.tensor.transpose(xts[i][:, g, u, :], words[:, u : D // 2 : 2], ident[:])
 
@@ -152,7 +148,7 @@ def tile_heterogeneousgraphtransformer_pb_s_kernel(
             nc.vector.tensor_tensor(out=resid[i][:], in0=scene_view(i), in1=bo_ps[:], op=ALU.add)
 
         def residual_on_gpsimd(i):
-            resid[i] = keep.tile([P, D], F32, name="grouped%d" % {1: 2, 3: 3}[i], align_bytes=64)
+            resid[i] = keep.tile([P, D], F32, name="grouped2", align_bytes=64)
             nc.gpsimd.tensor_tensor(out=resid[i][:], in0=scene_view(i), in1=bo_sb[:], op=ALU.add)
 
         def add_residual(i):
@@ -207,26 +203,27 @@ def tile_heterogeneousgraphtransformer_pb_s_kernel(
             store(nc.sync, i, result)
 
         dummies(2)
-        bo_ps = spread(bo_rows, "bo_ps")
-        residual_on_vector(0)
-        residual_on_vector(2)
         transpose(0)
+        bo_ps = spread(bo_rows, "bo_ps")
         transpose(2)
         dummies(2)
+        residual_on_vector(0)
         regroup(0)
+        quantise(0)
+        residual_on_vector(2)
         regroup(2)
         bo_sb = keep.tile([P, D], BF16)
         nc.scalar.copy(out=bo_sb[:], in_=bo_ps[:])
-        quantise(0)
         quantise(2)
         multiply(0)
         transpose(1)
         multiply(2)
         gamma_ps = spread(gamma_rows, "gamma_ps")
         transpose(3)
-        residual_on_gpsimd(1)
+        residual_on_gpsimd(3)
 
         add_residual(0)
+        residual_on_vector(1)
         regroup(1)
         negative_mean(0)
         squares_of(0)
@@ -235,7 +232,6 @@ def tile_heterogeneousgraphtransformer_pb_s_kernel(
         quantise(1)
         centre_and_gamma(0)
         quantise(3)
-        residual_on_gpsimd(3)
         multiply(1)
         multiply(3)
         negative_mean(2)
@@ -244,12 +240,12 @@ def tile_heterogeneousgraphtransformer_pb_s_kernel(
         add_residual(1)
         reciprocal_std(0)
         finish_on_scalar_and_gpsimd(0)
-        negative_mean(1)
         reciprocal_std(2)
         finish_on_scalar_and_gpsimd(2)
-        squares_of(1)
+        negative_mean(1)
         add_residual(3)
         negative_mean(3)
+        squares_of(1)
         reciprocal_std(1)
         squares_of(3)
         reciprocal_std(3)

@@ -229,17 +229,17 @@ def tile_heterogeneousgraphtransformer_pb_s_kernel(
         squares_of(0)
         regroup(3)
         add_residual(2)
-        quantise(1)
         centre_and_gamma(0)
+        quantise(1)
         quantise(3)
         multiply(1)
         multiply(3)
         negative_mean(2)
+        reciprocal_std(0)
+        finish_on_scalar_and_gpsimd(0)
         squares_of(2)
         centre_and_gamma(2)
         add_residual(1)
-        reciprocal_std(0)
-        finish_on_scalar_and_gpsimd(0)
         reciprocal_std(2)
         finish_on_scalar_and_gpsimd(2)
         negative_mean(1)

@@ -50,7 +50,7 @@ def tile_heterogeneousgraphtransformer_pb_s_kernel(
         att_blocks = att[:, 0, :, :].rearrange("e (i s) d -> s (e i) d", s=P)
         scene_blocks = scene_reps[0, :, :].rearrange("(i s) d -> s i d", s=P)
         att_sb = [keep.tile([P, E, D], BF16, name="att%d" % i) for i in range(ROW_TILES)]
-        scene_even = keep.tile([P, 2, D], BF16)
+        scene_one = {i: keep.tile([P, D], BF16, name="scene%d" % i) for i in (0, 2)}
         scene_odd = keep.tile([P, 2, D], BF16)
         w_words = keep.tile([P, E, 2 * D], U8, align_bytes=64)
 
@@ -58,12 +58,14 @@ def tile_heterogeneousgraphtransformer_pb_s_kernel(
             nc.sync.dma_start(out=att_sb[i][:], in_=att_blocks[:, i : E * ROW_TILES : ROW_TILES, :])
 
         def scene_view(i):
-            return (scene_odd if i % 2 else scene_even)[:, i // 2, :]
+            return scene_odd[:, i // 2, :] if i % 2 else scene_one[i][:]
 
-        load_att(0)
+        for e in range(E):
+            nc.sync.dma_start(out=att_sb[0][:, e, :], in_=att_blocks[:, e * ROW_TILES, :])
         nc.sync.dma_start(out=bo_rows[0:1, :], in_=bo.unsqueeze(0))
-        nc.sync.dma_start(out=scene_even[:], in_=scene_blocks[:, 0:ROW_TILES:2, :])
+        nc.sync.dma_start(out=scene_one[0][:], in_=scene_blocks[:, 0, :])
         load_att(2)
+        nc.sync.dma_start(out=scene_one[2][:], in_=scene_blocks[:, 2, :])
         nc.sync.dma_start(
             out=w_words[:].bitcast(I32), in_=Wo_words.bitcast(I32).rearrange("g p w -> p g w")
         )
@@ -74,8 +76,8 @@ def tile_heterogeneousgraphtransformer_pb_s_kernel(
                 in_=scale_words[:, r:16:4, :].rearrange("g q w -> q g w"),
             )
         load_att(1)
-        load_att(3)
         nc.sync.dma_start(out=scene_odd[:], in_=scene_blocks[:, 1:ROW_TILES:2, :])
+        load_att(3)
         beta_sb = keep.tile([P, D], BF16)
         nc.sync.dma_start(out=beta_sb[:], in_=beta.partition_broadcast(P))
 
@@ -243,9 +245,9 @@ def tile_heterogeneousgraphtransformer_pb_s_kernel(
         reciprocal_std(2)
         finish_on_scalar_and_gpsimd(2)
         negative_mean(1)
+        squares_of(1)
         add_residual(3)
         negative_mean(3)
-        squares_of(1)
         reciprocal_std(1)
         squares_of(3)
         reciprocal_std(3)

@@ -145,6 +145,19 @@ def tile_heterogeneousgraphtransformer_pb_s_kernel(
                     stop=(g == E - 1),
                 )
 
+        def repeat_pass(i, count):
+            cols = slice((E - 1) * P, E * P)
+            for j in range(count):
+                nc.tensor.matmul_mx(
+                    out=warm_ps[:],
+                    lhsT=codes[i][:, cols].bitcast(FP8X4),
+                    lhsT_scale=planes[i][:, cols],
+                    rhs=w_words[:, E - 1, :].bitcast(FP4X4),
+                    rhs_scale=w_planes[:, E - 1, :],
+                    start=True,
+                    stop=True,
+                )
+
         def residual_on_vector(i):
             resid[i] = keep.tile([P, D], F32, name="resid%d" % i)
             nc.vector.tensor_tensor(out=resid[i][:], in0=scene_view(i), in1=bo_ps[:], op=ALU.add)
@@ -186,23 +199,29 @@ def tile_heterogeneousgraphtransformer_pb_s_kernel(
                 op0=ALU.add, op1=ALU.mult,
             )
 
-        def store(queue, i, result):
-            queue.dma_start(out=out[0, i * P : (i + 1) * P, :], in_=result[:])
+        halves = (slice(0, D // 2), slice(D // 2, D))
 
-        def finish_on_scalar_and_gpsimd(i):
+        def store(i, result, cols):
+            nc.sync.dma_start(out=out[0, i * P : (i + 1) * P, cols], in_=result[:, cols])
+
+        def finish_on_scalar_and_gpsimd(i, pieces):
             normed = keep.tile([P, D], F32, name="normed%d" % i)
-            nc.scalar.activation(out=normed[:], in_=scaled[i][:], func=ACT.Copy, scale=rstd[i][:])
             result = keep.tile([P, D], F32, name="result%d" % i)
-            nc.gpsimd.tensor_tensor(out=result[:], in0=normed[:], in1=beta_sb[:], op=ALU.add)
-            store(nc.sync, i, result)
+            for cols in pieces:
+                nc.scalar.activation(out=normed[:, cols], in_=scaled[i][:, cols], func=ACT.Copy, scale=rstd[i][:])
+                nc.gpsimd.tensor_tensor(
+                    out=result[:, cols], in0=normed[:, cols], in1=beta_sb[:, cols], op=ALU.add
+                )
+                store(i, result, cols)
 
-        def finish_on_vector(i):
+        def finish_on_vector(i, pieces):
             result = keep.tile([P, D], F32, name="result%d" % i)
-            nc.vector.scalar_tensor_tensor(
-                out=result[:], in0=scaled[i][:], scalar=rstd[i][:], in1=beta_sb[:],
-                op0=ALU.mult, op1=ALU.add,
-            )
-            store(nc.sync, i, result)
+            for cols in pieces:
+                nc.vector.scalar_tensor_tensor(
+                    out=result[:, cols], in0=scaled[i][:, cols], scalar=rstd[i][:], in1=beta_sb[:, cols],
+                    op0=ALU.mult, op1=ALU.add,
+                )
+                store(i, result, cols)
 
         dummies(2)
         transpose(0)
@@ -222,6 +241,7 @@ def tile_heterogeneousgraphtransformer_pb_s_kernel(
         multiply(2)
         gamma_ps = spread(gamma_rows, "gamma_ps")
         transpose(3)
+        repeat_pass(2, 2)
         residual_on_gpsimd(3)
 
         add_residual(0)
@@ -238,12 +258,12 @@ def tile_heterogeneousgraphtransformer_pb_s_kernel(
         multiply(3)
         negative_mean(2)
         reciprocal_std(0)
-        finish_on_scalar_and_gpsimd(0)
+        finish_on_scalar_and_gpsimd(0, (slice(0, D),))
         squares_of(2)
         centre_and_gamma(2)
         add_residual(1)
         reciprocal_std(2)
-        finish_on_scalar_and_gpsimd(2)
+        finish_on_scalar_and_gpsimd(2, halves)
         negative_mean(1)
         squares_of(1)
         add_residual(3)
@@ -253,5 +273,5 @@ def tile_heterogeneousgraphtransformer_pb_s_kernel(
         reciprocal_std(3)
         centre_and_gamma(1)
         centre_and_gamma(3)
-        finish_on_vector(1)
-        finish_on_vector(3)
+        finish_on_vector(1, (slice(0, D),))
+        finish_on_vector(3, halves)

from contextlib import ExitStack

import concourse.mybir as mybir
from concourse.masks import make_identity

F32 = mybir.dt.float32
BF16 = mybir.dt.bfloat16
I32 = mybir.dt.int32
U32 = mybir.dt.uint32
U8 = mybir.dt.uint8
FP8X4 = mybir.dt.float8_e4m3fn_x4
FP4X4 = mybir.dt.float4_e2m1fn_x4
ALU = mybir.AluOpType
ACT = mybir.ActivationFunctionType

P = 128
S = 512
D = 512
E = 2
ROW_TILES = S // P
EPS = 1e-5

FLOPS = 2 * S * (E * D) * D


def tile_heterogeneousgraphtransformer_pb_s_kernel(
    tc, att, scene_reps, Wo_words, Wo_scales, bo, gamma, beta, out
):
    nc = tc.nc
    with ExitStack() as ctx:
        keep = ctx.enter_context(tc.tile_pool(name="keep", bufs=1))
        psum_rows = ctx.enter_context(tc.psum_pool(name="psum_rows", bufs=1))
        psum_xt = ctx.enter_context(tc.psum_pool(name="psum_xt", bufs=2))
        psum_acc = ctx.enter_context(tc.psum_pool(name="psum_acc", bufs=3))
        ctx.enter_context(tc.manual_schedule())

        w_planes = keep.tile([P, E, D], U8, align_bytes=64)
        bo_rows = keep.tile([P, D], BF16)
        gamma_rows = keep.tile([P, D], BF16)
        ones = keep.tile([P, P], BF16)
        one_col = keep.tile([P, 1], F32)
        warm_in = keep.tile([P, P], F32)
        nc.vector.memset(bo_rows[:].bitcast(I32), 0)
        nc.vector.memset(warm_in[:], 0.0)
        nc.vector.memset(w_planes[:].rearrange("p g n -> p (g n)").bitcast(I32), 0)
        nc.vector.memset(ones[:], 1.0)
        nc.vector.memset(one_col[:], 1.0)
        nc.vector.memset(gamma_rows[:].bitcast(I32), 0)

        att_blocks = att[:, 0, :, :].rearrange("e (i s) d -> s (e i) d", s=P)
        scene_blocks = scene_reps[0, :, :].rearrange("(i s) d -> s i d", s=P)
        att_sb = [keep.tile([P, E, D], BF16, name="att%d" % i) for i in range(ROW_TILES)]
        scene_one = {i: keep.tile([P, D], BF16, name="scene%d" % i) for i in (0, 2)}
        scene_odd = keep.tile([P, 2, D], BF16)
        w_words = keep.tile([P, E, 2 * D], U8, align_bytes=64)

        def load_att(i):
            nc.sync.dma_start(out=att_sb[i][:], in_=att_blocks[:, i : E * ROW_TILES : ROW_TILES, :])

        def scene_view(i):
            return scene_odd[:, i // 2, :] if i % 2 else scene_one[i][:]

        for e in range(E):
            nc.sync.dma_start(out=att_sb[0][:, e, :], in_=att_blocks[:, e * ROW_TILES, :])
        nc.sync.dma_start(out=bo_rows[0:1, :], in_=bo.unsqueeze(0))
        nc.sync.dma_start(out=scene_one[0][:], in_=scene_blocks[:, 0, :])
        load_att(2)
        nc.sync.dma_start(out=scene_one[2][:], in_=scene_blocks[:, 2, :])
        nc.sync.dma_start(
            out=w_words[:].bitcast(I32), in_=Wo_words.bitcast(I32).rearrange("g p w -> p g w")
        )
        scale_words = Wo_scales.bitcast(I32)
        for r in range(4):
            nc.sync.dma_start(
                out=w_planes[r:P:32, :, :].bitcast(I32),
                in_=scale_words[:, r:16:4, :].rearrange("g q w -> q g w"),
            )
        load_att(1)
        nc.sync.dma_start(out=scene_odd[:], in_=scene_blocks[:, 1:ROW_TILES:2, :])
        load_att(3)
        beta_sb = keep.tile([P, D], BF16)
        nc.sync.dma_start(out=beta_sb[:], in_=beta.partition_broadcast(P))

        ident = keep.tile([P, P], F32)
        make_identity(nc, ident[:])
        nc.gpsimd.dma_start(out=gamma_rows[0:1, :], in_=gamma.unsqueeze(0))

        table_warm = keep.tile([P, 1], F32)
        nc.scalar.activation(out=table_warm[:], in_=one_col[:], func=ACT.Abs_reciprocal_sqrt)

        def spread(rows_tile, name):
            spread_ps = psum_rows.tile([P, D], F32, name=name)
            nc.tensor.matmul(out=spread_ps[:], lhsT=ones[:], rhs=rows_tile[:], start=True, stop=True)
            return spread_ps

        warm_ps = psum_rows.tile([P, D], F32, name="warm_ps")

        def dummies(count):
            for j in range(count):
                nc.tensor.matmul(out=warm_ps[:, 0:P], lhsT=warm_in[:], rhs=warm_in[:], start=True, stop=True)

        xts = {}
        grouped = {}
        codes = {}
        planes = {}
        acc = {}
        resid = {}
        y = {}
        y_sum = {}
        sq_sum = {}
        negmean = {}
        rstd = {}
        scaled = {}

        def transpose(i):
            xts[i] = psum_xt.tile([P, E, 2, P], F32, name="xt")
            for g in range(E):
                words = att_sb[i][:, g, :].bitcast(F32)
                for u in range(2):
                    nc.tensor.transpose(xts[i][:, g, u, :], words[:, u : D // 2 : 2], ident[:])

        def regroup(i):
            grouped[i] = keep.tile([P, E * P * 4], BF16, name="grouped%d" % i, align_bytes=64)
            nc.scalar.copy(
                out=grouped[i][:].bitcast(F32).rearrange("p (g s u) -> p g s u", g=E, u=2),
                in_=xts[i][:].rearrange("p g u s -> p g s u"),
            )

        def quantise(i):
            codes[i] = keep.tile([P, E * P], U32, name="codes%d" % i, align_bytes=64)
            planes[i] = keep.tile([P, E * P], U8, name="planes%d" % i, align_bytes=64)
            nc.vector.quantize_mx(out=codes[i][:].bitcast(FP8X4), scales=planes[i][:], in_=grouped[i][:])

        def multiply(i):
            acc[i] = psum_acc.tile([P, D], F32, name="acc")
            for g in range(E):
                cols = slice(g * P, (g + 1) * P)
                nc.tensor.matmul_mx(
                    out=acc[i][:],
                    lhsT=codes[i][:, cols].bitcast(FP8X4),
                    lhsT_scale=planes[i][:, cols],
                    rhs=w_words[:, g, :].bitcast(FP4X4),
                    rhs_scale=w_planes[:, g, :],
                    start=(g == 0),
                    stop=(g == E - 1),
                )

        def repeat_pass(i, count):
            cols = slice((E - 1) * P, E * P)
            for j in range(count):
                nc.tensor.matmul_mx(
                    out=warm_ps[:],
                    lhsT=codes[i][:, cols].bitcast(FP8X4),
                    lhsT_scale=planes[i][:, cols],
                    rhs=w_words[:, E - 1, :].bitcast(FP4X4),
                    rhs_scale=w_planes[:, E - 1, :],
                    start=True,
                    stop=True,
                )

        def residual_on_vector(i):
            resid[i] = keep.tile([P, D], F32, name="resid%d" % i)
            nc.vector.tensor_tensor(out=resid[i][:], in0=scene_view(i), in1=bo_ps[:], op=ALU.add)

        def residual_on_gpsimd(i):
            resid[i] = keep.tile([P, D], F32, name="grouped2", align_bytes=64)
            nc.gpsimd.tensor_tensor(out=resid[i][:], in0=scene_view(i), in1=bo_sb[:], op=ALU.add)

        def add_residual(i):
            y[i] = keep.tile([P, D], F32, name="y%d" % i)
            y_sum[i] = keep.tile([P, 1], F32, name="ysum%d" % i)
            nc.vector.scalar_tensor_tensor(
                out=y[i][:], in0=acc[i][:], scalar=1.0, in1=resid[i][:],
                op0=ALU.mult, op1=ALU.add, accum_out=y_sum[i][:],
            )

        def negative_mean(i):
            negmean[i] = keep.tile([P, 1], F32, name="negmean%d" % i)
            nc.scalar.activation(out=negmean[i][:], in_=y_sum[i][:], func=ACT.Copy, scale=-1.0 / D)

        def squares_of(i):
            squares = keep.tile([P, D], F32, name="squares%d" % i)
            sq_sum[i] = keep.tile([P, 1], F32, name="sqsum%d" % i)
            nc.scalar.activation(
                out=squares[:], in_=y[i][:], func=ACT.Square, bias=y_sum[i][:], scale=-float(D),
                accum_out=sq_sum[i][:],
            )

        def reciprocal_std(i):
            rstd[i] = keep.tile([P, 1], F32, name="rstd%d" % i)
            nc.scalar.activation(
                out=rstd[i][:], in_=sq_sum[i][:], func=ACT.Abs_reciprocal_sqrt, bias=EPS, scale=1.0 / D**3
            )

        def centre_and_gamma(i):
            scaled[i] = keep.tile([P, D], F32, name="scaled%d" % i)
            nc.vector.scalar_tensor_tensor(
                out=scaled[i][:], in0=y[i][:], scalar=negmean[i][:], in1=gamma_ps[:],
                op0=ALU.add, op1=ALU.mult,
            )

        halves = (slice(0, D // 2), slice(D // 2, D))

        def store(i, result, cols):
            nc.sync.dma_start(out=out[0, i * P : (i + 1) * P, cols], in_=result[:, cols])

        def finish_on_scalar_and_gpsimd(i, pieces):
            normed = keep.tile([P, D], F32, name="normed%d" % i)
            result = keep.tile([P, D], F32, name="result%d" % i)
            for cols in pieces:
                nc.scalar.activation(out=normed[:, cols], in_=scaled[i][:, cols], func=ACT.Copy, scale=rstd[i][:])
                nc.gpsimd.tensor_tensor(
                    out=result[:, cols], in0=normed[:, cols], in1=beta_sb[:, cols], op=ALU.add
                )
                store(i, result, cols)

        def finish_on_vector(i, pieces):
            result = keep.tile([P, D], F32, name="result%d" % i)
            for cols in pieces:
                nc.vector.scalar_tensor_tensor(
                    out=result[:, cols], in0=scaled[i][:, cols], scalar=rstd[i][:], in1=beta_sb[:, cols],
                    op0=ALU.mult, op1=ALU.add,
                )
                store(i, result, cols)

        dummies(2)
        transpose(0)
        bo_ps = spread(bo_rows, "bo_ps")
        transpose(2)
        dummies(2)
        residual_on_vector(0)
        regroup(0)
        quantise(0)
        residual_on_vector(2)
        regroup(2)
        bo_sb = keep.tile([P, D], BF16)
        nc.scalar.copy(out=bo_sb[:], in_=bo_ps[:])
        quantise(2)
        multiply(0)
        transpose(1)
        multiply(2)
        gamma_ps = spread(gamma_rows, "gamma_ps")
        transpose(3)
        repeat_pass(2, 2)
        residual_on_gpsimd(3)

        add_residual(0)
        residual_on_vector(1)
        regroup(1)
        negative_mean(0)
        squares_of(0)
        regroup(3)
        add_residual(2)
        centre_and_gamma(0)
        quantise(1)
        quantise(3)
        multiply(1)
        multiply(3)
        negative_mean(2)
        reciprocal_std(0)
        finish_on_scalar_and_gpsimd(0, (slice(0, D),))
        squares_of(2)
        centre_and_gamma(2)
        add_residual(1)
        reciprocal_std(2)
        finish_on_scalar_and_gpsimd(2, halves)
        negative_mean(1)
        squares_of(1)
        add_residual(3)
        negative_mean(3)
        reciprocal_std(1)
        squares_of(3)
        reciprocal_std(3)
        centre_and_gamma(1)
        centre_and_gamma(3)
        finish_on_vector(1, (slice(0, D),))
        finish_on_vector(3, halves)
